import numpy as np
import ml_dtypes


def mxq(x, axis, fmt="e4m3"):
    dtype, down = {"e4m3": (ml_dtypes.float8_e4m3fn, 7), "e5m2": (ml_dtypes.float8_e5m2, 14)}[fmt]
    v = np.moveaxis(np.asarray(x, np.float32).astype(ml_dtypes.bfloat16).astype(np.float64), axis, -1)
    blocks = v.reshape(v.shape[:-1] + (-1, 32))
    amax = np.abs(blocks).max(-1, keepdims=True)
    byte = np.maximum(np.where(amax > 0, np.frexp(amax)[1] - 1 + 127, 0) - down, 1)
    scale = np.exp2(byte - 127.0)
    codes = (blocks / scale).astype(np.float32).astype(dtype).astype(np.float64)
    return np.moveaxis((codes * scale).reshape(v.shape), -1, axis)


WIDE = False


def mx_kscale(k):
    if not WIDE:
        return np.ones(k)
    levels = np.array([10, -10, 5, -5, 0])
    a = np.random.permutation(np.resize(levels, k // 512 * 4)).reshape(k // 512, 4)
    idx = np.arange(k)
    return np.exp2(a[idx // 512, idx % 128 // 32])


BF16 = ml_dtypes.bfloat16


def bf(x):
    return np.asarray(x, np.float32).astype(BF16)


def f64(x):
    return np.asarray(x).astype(np.float64)


E2M1 = np.array([0.0, 0.5, 1.0, 1.5, 2.0, 3.0, 4.0, 6.0, -0.0, -0.5, -1.0, -1.5, -2.0, -3.0, -4.0, -6.0])


def pack_weight(w, fmt):
    k, n = w.shape
    w = f64(bf(w)).reshape(k // 32, 32, n)
    amax = np.abs(w).max(1)
    if fmt == "e4m3":
        byte = np.frexp(amax)[1] - 1 + 127 - 7
    else:
        mant, ex = np.frexp(amax / 6.0)
        byte = np.where(mant > 0.5, ex, ex - 1) + 127
    byte = np.clip(np.where(amax > 0, byte, 1), 1, 254)
    scaled = (w * np.exp2(127.0 - byte)[:, None, :]).reshape(k, n).astype(np.float32)
    by_word = np.ascontiguousarray(scaled.reshape(k // 512, 128, 4, n).transpose(0, 1, 3, 2))
    if fmt == "e4m3":
        words = by_word.astype(ml_dtypes.float8_e4m3fn).view(np.uint8)
    else:
        c = by_word.astype(ml_dtypes.float4_e2m1fn).view(np.uint8) & 0xF
        words = c[..., 0::2] | (c[..., 1::2] << 4)
    return np.ascontiguousarray(words), np.ascontiguousarray(byte.astype(np.uint8).reshape(k // 512, 16, n))


def unpack_weight(words, scales, fmt):
    g, p, n, _ = words.shape
    if fmt == "e4m3":
        vals = np.ascontiguousarray(words).view(ml_dtypes.float8_e4m3fn).astype(np.float64)
    else:
        nib = np.empty((g, p, n, 4), np.uint8)
        nib[..., 0::2] = words & 0xF
        nib[..., 1::2] = words >> 4
        vals = E2M1[nib]
    vals = vals * np.repeat(np.exp2(scales.astype(np.float64) - 127.0), 8, axis=1)[..., None]
    return vals.transpose(0, 1, 3, 2).reshape(g * 512, n)

def pack4(w):
    words, scales = pack_weight(w, "e2m1")
    return words.reshape(words.shape[0], 128, -1), scales


def unpack4(words, scales):
    return unpack_weight(words.reshape(words.shape[0], 128, -1, 2), scales, "e2m1")


B, K, F, INCH, OUTCH, R = 2, 4, 128, 2048, 2048, 128


def erf(a):
    c = np.clip(a, -6.0, 6.0)
    c2 = 2.0 * c * c
    t = c.copy()
    s = c.copy()
    n = 1.0
    while np.max(np.abs(t) - 1e-18 * np.abs(s)) > 0.0:
        n += 2.0
        t = t * c2 / n
        s = s + t
    return 2.0 / np.sqrt(np.pi) * np.exp(-c * c) * s


def gelu(t):
    return 0.5 * t * (1.0 + erf(t / np.sqrt(2.0)))


def setup_inputs():
    s = mx_kscale(INCH)
    h = bf(gelu(np.random.standard_normal((B, K, F, INCH))) * s)
    z = bf(np.random.standard_normal((B, K, F, R)) * 0.35)
    u = bf(np.random.standard_normal((B, K, OUTCH, R)) * 1.5 * np.sqrt(R))
    b = bf(np.random.standard_normal((B, 1, 1, OUTCH)) * 0.3)
    w = np.random.standard_normal((OUTCH, INCH)) * 1.5 / np.sqrt(INCH) / s
    words, scales = pack4(np.ascontiguousarray(w.T))
    b_out = bf(np.random.standard_normal(OUTCH) * 0.3)
    return {
        "h": h,
        "z": z,
        "u": u,
        "b": b,
        "W_out_words": words,
        "W_out_scales": scales,
        "b_out": b_out,
    }


def reference(h, z, u, b, W_out_words, W_out_scales, b_out):
    lora = f64(z) @ f64(u).transpose(0, 1, 3, 2) / R
    main = mxq(f64(h), 3, "e4m3") @ unpack4(W_out_words, W_out_scales)
    return gelu(main + f64(b_out) + lora + f64(b))

@@ -1,0 +1,213 @@
+from contextlib import ExitStack
+
+import concourse.mybir as mybir
+from concourse.masks import make_identity
+
+BF16 = mybir.dt.bfloat16
+F32 = mybir.dt.float32
+I32 = mybir.dt.int32
+U8 = mybir.dt.uint8
+U32 = mybir.dt.uint32
+FP8X4 = mybir.dt.float8_e4m3fn_x4
+FP4X4 = mybir.dt.float4_e2m1fn_x4
+ADD = mybir.AluOpType.add
+MULT = mybir.AluOpType.mult
+GELU = mybir.ActivationFunctionType.Gelu
+
+P = 128
+BATCHES = 2
+MEMBERS = 4
+ROW_TILES = BATCHES * MEMBERS
+IN_CH = 2048
+OUT_CH = 2048
+RANK = 128
+PACK = 4
+K_PASS = P * PACK
+PASSES = IN_CH // K_PASS
+N_CHUNK = 512
+CHUNKS = OUT_CH // N_CHUNK
+LANES = N_CHUNK // P
+PAIR = 2
+
+FLOPS = 2 * ROW_TILES * P * OUT_CH * (IN_CH + RANK)
+
+
+def tile_loratacmlp4_pb_kernel(tc, h, z, u, b, W_out_words, W_out_scales, b_out, out):
+    nc = tc.nc
+    h_rows = h.rearrange("b k f c -> (b k) f c")
+    out_rows = out.rearrange("b k f n -> (b k) f n")
+    u_rows = u.rearrange("b k (a p j) r -> (b k) p a j r", a=CHUNKS, p=P)
+
+    with ExitStack() as ctx:
+        resident = ctx.enter_context(tc.tile_pool(name="resident", bufs=1))
+        stage = ctx.enter_context(tc.tile_pool(name="stage", bufs=2))
+        work = ctx.enter_context(tc.tile_pool(name="work", bufs=3))
+        results = ctx.enter_context(tc.tile_pool(name="results", bufs=12))
+        psum = ctx.enter_context(tc.psum_pool(name="psum", bufs=2))
+        ctx.enter_context(tc.manual_schedule())
+
+        w_planes = resident.tile([P, PASSES, OUT_CH], U8, align_bytes=64)
+        nc.vector.memset(w_planes[:].bitcast(I32), 0)
+        bias_rows = resident.tile([P, BATCHES, OUT_CH], BF16)
+        nc.vector.memset(bias_rows[:], 0.0)
+        ones = resident.tile([P, P], BF16)
+        nc.vector.memset(ones[:], 1.0)
+        ident_f32 = resident.tile([P, P], F32)
+        make_identity(nc, ident_f32[:])
+        ident_bf16 = resident.tile([P, P], BF16)
+        make_identity(nc, ident_bf16[:])
+
+        z_sb = resident.tile([P, ROW_TILES, RANK], BF16)
+        nc.scalar.dma_start(out=z_sb[:], in_=z.rearrange("b k f r -> f (b k) r"))
+        for bb in range(BATCHES):
+            nc.scalar.dma_start(out=bias_rows[0:1, bb, :], in_=b_out.unsqueeze(0))
+        nc.scalar.dma_start(out=bias_rows[1:2, :, :], in_=b.rearrange("b x y n -> (x y) b n"))
+        warm = resident.tile([P, 1], F32)
+        nc.scalar.activation(out=warm[:], in_=ones[:, 0:1], func=GELU)
+
+        h_sb = [resident.tile([P, IN_CH], BF16, name="h_sb%d" % i) for i in range(ROW_TILES)]
+        u_sb = [resident.tile([P, CHUNKS, LANES, RANK], BF16, name="u_sb%d" % i) for i in range(ROW_TILES)]
+        w_words = [
+            resident.tile([P, PASSES, 2 * N_CHUNK], U8, name="w_words%d" % a, align_bytes=64)
+            for a in range(CHUNKS)
+        ]
+
+        def load_rows(i):
+            nc.sync.dma_start(out=h_sb[i][:], in_=h_rows[i])
+            nc.sync.dma_start(out=u_sb[i][:], in_=u_rows[i])
+
+        def load_weight_chunk(a):
+            words = W_out_words.bitcast(I32).rearrange("g p n -> p g n")
+            width = 2 * N_CHUNK // 4
+            nc.sync.dma_start(out=w_words[a][:].bitcast(I32), in_=words[:, :, a * width : (a + 1) * width])
+
+        def load_weight_scales():
+            rows = W_out_scales.bitcast(I32).rearrange("g q n -> q g n")
+            for quadrant in range(2):
+                for r in range(4):
+                    nc.sync.dma_start(
+                        out=w_planes[32 * quadrant + r : P : 64, :, :].bitcast(I32),
+                        in_=rows[4 * quadrant + r : 16 : 8, :, :],
+                    )
+
+        load_rows(0)
+        load_weight_scales()
+        load_weight_chunk(0)
+        load_rows(1)
+        for a in range(1, CHUNKS):
+            load_weight_chunk(a)
+        for i in range(2, ROW_TILES):
+            load_rows(i)
+
+        def transpose_h(i):
+            words = h_sb[i][:].bitcast(F32)
+            per_pass = K_PASS // PAIR
+            grouped = stage.tile([P, PASSES, P, PACK], BF16, align_bytes=64)
+            grouped_words = grouped[:].bitcast(F32)
+            for half in range(PASSES // 2):
+                ht = psum.tile([P, 2, PAIR, P], F32)
+                for gg in range(2):
+                    g = 2 * half + gg
+                    for w in range(PAIR):
+                        nc.tensor.transpose(
+                            ht[:, gg, w, :],
+                            words[:, per_pass * g + w : per_pass * (g + 1) : PAIR],
+                            ident_f32[:],
+                        )
+                nc.scalar.copy(
+                    out=grouped_words[:, 2 * half : 2 * half + 2, :, :],
+                    in_=ht[:].rearrange("p g w f -> p g f w"),
+                )
+            return grouped
+
+        def quantise_h(grouped):
+            codes = stage.tile([P, PASSES * P], U32, align_bytes=64)
+            scales = stage.tile([P, PASSES * P], U8, align_bytes=64)
+            nc.vector.quantize_mx(
+                out=codes[:].bitcast(FP8X4),
+                scales=scales[:],
+                in_=grouped[:].rearrange("p g f t -> p (g f t)"),
+            )
+            return codes, scales
+
+        def transpose_z():
+            zt = psum.tile([P, ROW_TILES, P], BF16, tag="ut")
+            for i in range(ROW_TILES):
+                nc.tensor.transpose(zt[:, i, :], z_sb[:, i, :], ident_bf16[:])
+            z_t = resident.tile([P, ROW_TILES, P], BF16)
+            nc.scalar.copy(out=z_t[:], in_=zt[:])
+            return z_t
+
+        def transpose_u(i):
+            u_t = stage.tile([P, CHUNKS, LANES, P], BF16)
+            for half in range(CHUNKS // 2):
+                ut = psum.tile([P, 2, LANES, P], BF16)
+                for aa in range(2):
+                    for j in range(LANES):
+                        nc.tensor.transpose(ut[:, aa, j, :], u_sb[i][:, 2 * half + aa, j, :], ident_bf16[:])
+                nc.scalar.copy(out=u_t[:, 2 * half : 2 * half + 2, :, :], in_=ut[:])
+            return u_t
+
+        bias = {}
+
+        def spread_bias(bb, a):
+            spread = psum.tile([P, N_CHUNK], F32, tag="low_rank")
+            nc.tensor.matmul(
+                spread[:], lhsT=ones[:], rhs=bias_rows[:, bb, a * N_CHUNK : (a + 1) * N_CHUNK], start=True, stop=True
+            )
+            bias[bb, a] = resident.tile([P, N_CHUNK], F32, name="bias%d_%d" % (bb, a))
+            nc.scalar.copy(out=bias[bb, a][:], in_=spread[:])
+
+        def chunk(i, a, z_t, u_t, codes, scales):
+            bb = i // MEMBERS
+            low_rank = psum.tile([P, N_CHUNK], F32)
+            nc.tensor.matmul(
+                low_rank[:],
+                lhsT=z_t[:, i, :],
+                rhs=u_t[:, a, :, :].rearrange("r j p -> r (j p)"),
+                start=True,
+                stop=True,
+            )
+            acc = psum.tile([P, N_CHUNK], F32)
+            for g in range(PASSES):
+                nc.tensor.matmul_mx(
+                    out=acc[:],
+                    lhsT=codes[:, g * P : (g + 1) * P].bitcast(FP8X4),
+                    lhsT_scale=scales[:, g * P : (g + 1) * P],
+                    rhs=w_words[a][:, g, :].bitcast(FP4X4),
+                    rhs_scale=w_planes[:, g, a * N_CHUNK : (a + 1) * N_CHUNK],
+                    start=(g == 0),
+                    stop=(g == PASSES - 1),
+                )
+            added = work.tile([P, N_CHUNK], F32)
+            nc.vector.scalar_tensor_tensor(
+                out=added[:].rearrange("f (p j) -> f p j", j=LANES),
+                in0=low_rank[:].rearrange("f (j p) -> f p j", j=LANES),
+                scalar=1.0 / RANK,
+                in1=bias[bb, a][:].rearrange("f (p j) -> f p j", j=LANES),
+                op0=MULT,
+                op1=ADD,
+            )
+            total = work.tile([P, N_CHUNK], F32)
+            nc.vector.tensor_tensor(out=total[:], in0=acc[:], in1=added[:], op=ADD)
+            result = results.tile([P, N_CHUNK], F32)
+            nc.scalar.activation(out=result[:], in_=total[:], func=GELU)
+            nc.sync.dma_start(out=out_rows[i][:, a * N_CHUNK : (a + 1) * N_CHUNK], in_=result[:])
+
+        grouped = transpose_h(0)
+        z_t = transpose_z()
+        u_t = transpose_u(0)
+        codes, scales = quantise_h(grouped)
+        for i in range(ROW_TILES):
+            for a in range(CHUNKS):
+                if i % MEMBERS == 0:
+                    spread_bias(i // MEMBERS, a)
+                chunk(i, a, z_t, u_t, codes, scales)
+                if i + 1 < ROW_TILES:
+                    if a == 0:
+                        grouped = transpose_h(i + 1)
+                        next_u_t = transpose_u(i + 1)
+                    if a == 1:
+                        next_codes, next_scales = quantise_h(grouped)
+            if i + 1 < ROW_TILES:
+                u_t, codes, scales = next_u_t, next_codes, next_scales

@@ -28,6 +28,7 @@ N_CHUNK = 512
 CHUNKS = OUT_CH // N_CHUNK
 LANES = N_CHUNK // P
 PAIR = 2
+HALVES = 2
 
 FLOPS = 2 * ROW_TILES * P * OUT_CH * (IN_CH + RANK)
 
@@ -46,24 +47,26 @@ def tile_loratacmlp4_pb_kernel(tc, h, z, u, b, W_out_words, W_out_scales, b_out,
         psum = ctx.enter_context(tc.psum_pool(name="psum", bufs=2))
         ctx.enter_context(tc.manual_schedule())
 
+        warm_in = resident.tile([P, 1], F32)
+        nc.vector.memset(warm_in[:], 0.0)
         w_planes = resident.tile([P, PASSES, OUT_CH], U8, align_bytes=64)
         nc.vector.memset(w_planes[:].bitcast(I32), 0)
-        bias_rows = resident.tile([P, BATCHES, OUT_CH], BF16)
-        nc.vector.memset(bias_rows[:], 0.0)
         ones = resident.tile([P, P], BF16)
         nc.vector.memset(ones[:], 1.0)
         ident_f32 = resident.tile([P, P], F32)
         make_identity(nc, ident_f32[:])
+        bias_rows = resident.tile([P, BATCHES, OUT_CH], BF16)
+        nc.gpsimd.memset(bias_rows[:].bitcast(F32), 0.0)
         ident_bf16 = resident.tile([P, P], BF16)
         make_identity(nc, ident_bf16[:])
 
         z_sb = resident.tile([P, ROW_TILES, RANK], BF16)
         nc.scalar.dma_start(out=z_sb[:], in_=z.rearrange("b k f r -> f (b k) r"))
+        warm_out = resident.tile([P, 1], F32)
+        nc.scalar.activation(out=warm_out[:], in_=warm_in[:], func=GELU)
         for bb in range(BATCHES):
             nc.scalar.dma_start(out=bias_rows[0:1, bb, :], in_=b_out.unsqueeze(0))
         nc.scalar.dma_start(out=bias_rows[1:2, :, :], in_=b.rearrange("b x y n -> (x y) b n"))
-        warm = resident.tile([P, 1], F32)
-        nc.scalar.activation(out=warm[:], in_=ones[:, 0:1], func=GELU)
 
         h_sb = [resident.tile([P, IN_CH], BF16, name="h_sb%d" % i) for i in range(ROW_TILES)]
         u_sb = [resident.tile([P, CHUNKS, LANES, RANK], BF16, name="u_sb%d" % i) for i in range(ROW_TILES)]
@@ -99,26 +102,27 @@ def tile_loratacmlp4_pb_kernel(tc, h, z, u, b, W_out_words, W_out_scales, b_out,
         for i in range(2, ROW_TILES):
             load_rows(i)
 
-        def transpose_h(i):
+        def new_stage_tiles():
+            grouped = stage.tile([P, PASSES, P, PACK], BF16, align_bytes=64)
+            u_t = stage.tile([P, CHUNKS, LANES, P], BF16)
+            return grouped, u_t
+
+        def transpose_h(i, half, grouped):
             words = h_sb[i][:].bitcast(F32)
             per_pass = K_PASS // PAIR
-            grouped = stage.tile([P, PASSES, P, PACK], BF16, align_bytes=64)
-            grouped_words = grouped[:].bitcast(F32)
-            for half in range(PASSES // 2):
-                ht = psum.tile([P, 2, PAIR, P], F32)
-                for gg in range(2):
-                    g = 2 * half + gg
-                    for w in range(PAIR):
-                        nc.tensor.transpose(
-                            ht[:, gg, w, :],
-                            words[:, per_pass * g + w : per_pass * (g + 1) : PAIR],
-                            ident_f32[:],
-                        )
-                nc.scalar.copy(
-                    out=grouped_words[:, 2 * half : 2 * half + 2, :, :],
-                    in_=ht[:].rearrange("p g w f -> p g f w"),
-                )
-            return grouped
+            ht = psum.tile([P, 2, PAIR, P], F32)
+            for gg in range(2):
+                g = 2 * half + gg
+                for w in range(PAIR):
+                    nc.tensor.transpose(
+                        ht[:, gg, w, :],
+                        words[:, per_pass * g + w : per_pass * (g + 1) : PAIR],
+                        ident_f32[:],
+                    )
+            nc.scalar.copy(
+                out=grouped[:].bitcast(F32)[:, 2 * half : 2 * half + 2, :, :],
+                in_=ht[:].rearrange("p g w f -> p g f w"),
+            )
 
         def quantise_h(grouped):
             codes = stage.tile([P, PASSES * P], U32, align_bytes=64)
@@ -138,15 +142,12 @@ def tile_loratacmlp4_pb_kernel(tc, h, z, u, b, W_out_words, W_out_scales, b_out,
             nc.scalar.copy(out=z_t[:], in_=zt[:])
             return z_t
 
-        def transpose_u(i):
-            u_t = stage.tile([P, CHUNKS, LANES, P], BF16)
-            for half in range(CHUNKS // 2):
-                ut = psum.tile([P, 2, LANES, P], BF16)
-                for aa in range(2):
-                    for j in range(LANES):
-                        nc.tensor.transpose(ut[:, aa, j, :], u_sb[i][:, 2 * half + aa, j, :], ident_bf16[:])
-                nc.scalar.copy(out=u_t[:, 2 * half : 2 * half + 2, :, :], in_=ut[:])
-            return u_t
+        def transpose_u(i, half, u_t):
+            ut = psum.tile([P, 2, LANES, P], BF16)
+            for aa in range(2):
+                for j in range(LANES):
+                    nc.tensor.transpose(ut[:, aa, j, :], u_sb[i][:, 2 * half + aa, j, :], ident_bf16[:])
+            nc.scalar.copy(out=u_t[:, 2 * half : 2 * half + 2, :, :], in_=ut[:])
 
         bias = {}
 
@@ -158,8 +159,7 @@ def tile_loratacmlp4_pb_kernel(tc, h, z, u, b, W_out_words, W_out_scales, b_out,
             bias[bb, a] = resident.tile([P, N_CHUNK], F32, name="bias%d_%d" % (bb, a))
             nc.scalar.copy(out=bias[bb, a][:], in_=spread[:])
 
-        def chunk(i, a, z_t, u_t, codes, scales):
-            bb = i // MEMBERS
+        def multiply_low_rank(i, a, z_t, u_t):
             low_rank = psum.tile([P, N_CHUNK], F32)
             nc.tensor.matmul(
                 low_rank[:],
@@ -168,6 +168,10 @@ def tile_loratacmlp4_pb_kernel(tc, h, z, u, b, W_out_words, W_out_scales, b_out,
                 start=True,
                 stop=True,
             )
+            return low_rank
+
+        def finish_chunk(i, a, low_rank, codes, scales):
+            bb = i // MEMBERS
             acc = psum.tile([P, N_CHUNK], F32)
             for g in range(PASSES):
                 nc.tensor.matmul_mx(
@@ -194,20 +198,30 @@ def tile_loratacmlp4_pb_kernel(tc, h, z, u, b, W_out_words, W_out_scales, b_out,
             nc.scalar.activation(out=result[:], in_=total[:], func=GELU)
             nc.sync.dma_start(out=out_rows[i][:, a * N_CHUNK : (a + 1) * N_CHUNK], in_=result[:])
 
-        grouped = transpose_h(0)
+        grouped, u_t = new_stage_tiles()
+        for half in range(HALVES):
+            transpose_h(0, half, grouped)
         z_t = transpose_z()
-        u_t = transpose_u(0)
+        for half in range(HALVES):
+            transpose_u(0, half, u_t)
         codes, scales = quantise_h(grouped)
         for i in range(ROW_TILES):
+            following = i + 1 < ROW_TILES
             for a in range(CHUNKS):
                 if i % MEMBERS == 0:
                     spread_bias(i // MEMBERS, a)
-                chunk(i, a, z_t, u_t, codes, scales)
-                if i + 1 < ROW_TILES:
-                    if a == 0:
-                        grouped = transpose_h(i + 1)
-                        next_u_t = transpose_u(i + 1)
-                    if a == 1:
-                        next_codes, next_scales = quantise_h(grouped)
-            if i + 1 < ROW_TILES:
+                low_rank = multiply_low_rank(i, a, z_t, u_t)
+                if following and a == 0:
+                    grouped, next_u_t = new_stage_tiles()
+                    transpose_u(i + 1, 0, next_u_t)
+                if following and a == 1:
+                    transpose_h(i + 1, 0, grouped)
+                if following and a == 2:
+                    transpose_h(i + 1, 1, grouped)
+                if following and a == 3:
+                    transpose_u(i + 1, 1, next_u_t)
+                finish_chunk(i, a, low_rank, codes, scales)
+                if following and a == 2:
+                    next_codes, next_scales = quantise_h(grouped)
+            if following:
                 u_t, codes, scales = next_u_t, next_codes, next_scales

@@ -28,7 +28,6 @@ N_CHUNK = 512
 CHUNKS = OUT_CH // N_CHUNK
 LANES = N_CHUNK // P
 PAIR = 2
-HALVES = 2
 
 FLOPS = 2 * ROW_TILES * P * OUT_CH * (IN_CH + RANK)
 
@@ -43,22 +42,23 @@ def tile_loratacmlp4_pb_kernel(tc, h, z, u, b, W_out_words, W_out_scales, b_out,
         resident = ctx.enter_context(tc.tile_pool(name="resident", bufs=1))
         stage = ctx.enter_context(tc.tile_pool(name="stage", bufs=2))
         work = ctx.enter_context(tc.tile_pool(name="work", bufs=3))
+        addends = ctx.enter_context(tc.tile_pool(name="addends", bufs=2 * CHUNKS))
         results = ctx.enter_context(tc.tile_pool(name="results", bufs=12))
         psum = ctx.enter_context(tc.psum_pool(name="psum", bufs=2))
         ctx.enter_context(tc.manual_schedule())
 
         warm_in = resident.tile([P, 1], F32)
         nc.vector.memset(warm_in[:], 0.0)
-        w_planes = resident.tile([P, PASSES, OUT_CH], U8, align_bytes=64)
-        nc.vector.memset(w_planes[:].bitcast(I32), 0)
+        bias_rows = resident.tile([P, BATCHES, OUT_CH], BF16)
+        nc.vector.memset(bias_rows[:].bitcast(F32), 0.0)
         ones = resident.tile([P, P], BF16)
         nc.vector.memset(ones[:], 1.0)
-        ident_f32 = resident.tile([P, P], F32)
-        make_identity(nc, ident_f32[:])
-        bias_rows = resident.tile([P, BATCHES, OUT_CH], BF16)
-        nc.gpsimd.memset(bias_rows[:].bitcast(F32), 0.0)
+        w_planes = resident.tile([P, PASSES, OUT_CH], U8, align_bytes=64)
+        nc.vector.memset(w_planes[:].bitcast(I32), 0)
         ident_bf16 = resident.tile([P, P], BF16)
         make_identity(nc, ident_bf16[:])
+        ident_f32 = resident.tile([P, P], F32)
+        make_identity(nc, ident_f32[:])
 
         z_sb = resident.tile([P, ROW_TILES, RANK], BF16)
         nc.scalar.dma_start(out=z_sb[:], in_=z.rearrange("b k f r -> f (b k) r"))
@@ -94,10 +94,9 @@ def tile_loratacmlp4_pb_kernel(tc, h, z, u, b, W_out_words, W_out_scales, b_out,
                     )
 
         load_rows(0)
-        load_weight_scales()
-        load_weight_chunk(0)
         load_rows(1)
-        for a in range(1, CHUNKS):
+        load_weight_scales()
+        for a in range(CHUNKS):
             load_weight_chunk(a)
         for i in range(2, ROW_TILES):
             load_rows(i)
@@ -107,22 +106,32 @@ def tile_loratacmlp4_pb_kernel(tc, h, z, u, b, W_out_words, W_out_scales, b_out,
             u_t = stage.tile([P, CHUNKS, LANES, P], BF16)
             return grouped, u_t
 
-        def transpose_h(i, half, grouped):
+        def transpose_h(i, g, ht):
             words = h_sb[i][:].bitcast(F32)
             per_pass = K_PASS // PAIR
-            ht = psum.tile([P, 2, PAIR, P], F32)
-            for gg in range(2):
-                g = 2 * half + gg
-                for w in range(PAIR):
-                    nc.tensor.transpose(
-                        ht[:, gg, w, :],
-                        words[:, per_pass * g + w : per_pass * (g + 1) : PAIR],
-                        ident_f32[:],
-                    )
-            nc.scalar.copy(
-                out=grouped[:].bitcast(F32)[:, 2 * half : 2 * half + 2, :, :],
-                in_=ht[:].rearrange("p g w f -> p g f w"),
-            )
+            for w in range(PAIR):
+                nc.tensor.transpose(
+                    ht[:, g % 2, w, :],
+                    words[:, per_pass * g + w : per_pass * (g + 1) : PAIR],
+                    ident_f32[:],
+                )
+
+        def transpose_u(i, a, ut):
+            for j in range(LANES):
+                nc.tensor.transpose(ut[:, a % 2, j, :], u_sb[i][:, a, j, :], ident_bf16[:])
+
+        def transpose_quarter(i, quarter, banks, grouped, u_t):
+            if quarter % 2 == 0:
+                banks["ut"] = psum.tile([P, 2, LANES, P], BF16, name="ut")
+                banks["ht"] = psum.tile([P, 2, PAIR, P], F32, name="ht")
+            transpose_h(i, quarter, banks["ht"])
+            transpose_u(i, quarter, banks["ut"])
+            if quarter % 2 == 1:
+                nc.scalar.copy(out=u_t[:, quarter - 1 : quarter + 1, :, :], in_=banks["ut"][:])
+                nc.scalar.copy(
+                    out=grouped[:].bitcast(F32)[:, quarter - 1 : quarter + 1, :, :],
+                    in_=banks["ht"][:].rearrange("p g w f -> p g f w"),
+                )
 
         def quantise_h(grouped):
             codes = stage.tile([P, PASSES * P], U32, align_bytes=64)
@@ -134,21 +143,6 @@ def tile_loratacmlp4_pb_kernel(tc, h, z, u, b, W_out_words, W_out_scales, b_out,
             )
             return codes, scales
 
-        def transpose_z():
-            zt = psum.tile([P, ROW_TILES, P], BF16, tag="ut")
-            for i in range(ROW_TILES):
-                nc.tensor.transpose(zt[:, i, :], z_sb[:, i, :], ident_bf16[:])
-            z_t = resident.tile([P, ROW_TILES, P], BF16)
-            nc.scalar.copy(out=z_t[:], in_=zt[:])
-            return z_t
-
-        def transpose_u(i, half, u_t):
-            ut = psum.tile([P, 2, LANES, P], BF16)
-            for aa in range(2):
-                for j in range(LANES):
-                    nc.tensor.transpose(ut[:, aa, j, :], u_sb[i][:, 2 * half + aa, j, :], ident_bf16[:])
-            nc.scalar.copy(out=u_t[:, 2 * half : 2 * half + 2, :, :], in_=ut[:])
-
         bias = {}
 
         def spread_bias(bb, a):
@@ -157,7 +151,7 @@ def tile_loratacmlp4_pb_kernel(tc, h, z, u, b, W_out_words, W_out_scales, b_out,
                 spread[:], lhsT=ones[:], rhs=bias_rows[:, bb, a * N_CHUNK : (a + 1) * N_CHUNK], start=True, stop=True
             )
             bias[bb, a] = resident.tile([P, N_CHUNK], F32, name="bias%d_%d" % (bb, a))
-            nc.scalar.copy(out=bias[bb, a][:], in_=spread[:])
+            nc.vector.tensor_copy(out=bias[bb, a][:], in_=spread[:])
 
         def multiply_low_rank(i, a, z_t, u_t):
             low_rank = psum.tile([P, N_CHUNK], F32)
@@ -168,10 +162,18 @@ def tile_loratacmlp4_pb_kernel(tc, h, z, u, b, W_out_words, W_out_scales, b_out,
                 start=True,
                 stop=True,
             )
-            return low_rank
+            added = addends.tile([P, N_CHUNK], F32)
+            nc.vector.scalar_tensor_tensor(
+                out=added[:].rearrange("f (p j) -> f p j", j=LANES),
+                in0=low_rank[:].rearrange("f (j p) -> f p j", j=LANES),
+                scalar=1.0 / RANK,
+                in1=bias[i // MEMBERS, a][:].rearrange("f (p j) -> f p j", j=LANES),
+                op0=MULT,
+                op1=ADD,
+            )
+            return added
 
-        def finish_chunk(i, a, low_rank, codes, scales):
-            bb = i // MEMBERS
+        def multiply_mx(i, a, added, codes, scales):
             acc = psum.tile([P, N_CHUNK], F32)
             for g in range(PASSES):
                 nc.tensor.matmul_mx(
@@ -183,45 +185,37 @@ def tile_loratacmlp4_pb_kernel(tc, h, z, u, b, W_out_words, W_out_scales, b_out,
                     start=(g == 0),
                     stop=(g == PASSES - 1),
                 )
-            added = work.tile([P, N_CHUNK], F32)
-            nc.vector.scalar_tensor_tensor(
-                out=added[:].rearrange("f (p j) -> f p j", j=LANES),
-                in0=low_rank[:].rearrange("f (j p) -> f p j", j=LANES),
-                scalar=1.0 / RANK,
-                in1=bias[bb, a][:].rearrange("f (p j) -> f p j", j=LANES),
-                op0=MULT,
-                op1=ADD,
-            )
             total = work.tile([P, N_CHUNK], F32)
             nc.vector.tensor_tensor(out=total[:], in0=acc[:], in1=added[:], op=ADD)
             result = results.tile([P, N_CHUNK], F32)
             nc.scalar.activation(out=result[:], in_=total[:], func=GELU)
             nc.sync.dma_start(out=out_rows[i][:, a * N_CHUNK : (a + 1) * N_CHUNK], in_=result[:])
 
+        banks = {}
         grouped, u_t = new_stage_tiles()
-        for half in range(HALVES):
-            transpose_h(0, half, grouped)
-        z_t = transpose_z()
-        for half in range(HALVES):
-            transpose_u(0, half, u_t)
+        zt = psum.tile([P, ROW_TILES, P], BF16, tag="acc")
+        z_t = resident.tile([P, ROW_TILES, P], BF16)
+        for quarter in range(CHUNKS):
+            spread_bias(*divmod(2 * quarter, CHUNKS))
+            for i in (2 * quarter, 2 * quarter + 1):
+                nc.tensor.transpose(zt[:, i, :], z_sb[:, i, :], ident_bf16[:])
+            if quarter == CHUNKS - 1:
+                nc.scalar.copy(out=z_t[:], in_=zt[:])
+            spread_bias(*divmod(2 * quarter + 1, CHUNKS))
+            transpose_quarter(0, quarter, banks, grouped, u_t)
         codes, scales = quantise_h(grouped)
         for i in range(ROW_TILES):
             following = i + 1 < ROW_TILES
+            if following:
+                grouped, next_u_t = new_stage_tiles()
+            added = []
             for a in range(CHUNKS):
-                if i % MEMBERS == 0:
-                    spread_bias(i // MEMBERS, a)
-                low_rank = multiply_low_rank(i, a, z_t, u_t)
+                added.append(multiply_low_rank(i, a, z_t, u_t))
+                if following:
+                    transpose_quarter(i + 1, a, banks, grouped, next_u_t)
+            for a in range(CHUNKS):
+                multiply_mx(i, a, added[a], codes, scales)
                 if following and a == 0:
-                    grouped, next_u_t = new_stage_tiles()
-                    transpose_u(i + 1, 0, next_u_t)
-                if following and a == 1:
-                    transpose_h(i + 1, 0, grouped)
-                if following and a == 2:
-                    transpose_h(i + 1, 1, grouped)
-                if following and a == 3:
-                    transpose_u(i + 1, 1, next_u_t)
-                finish_chunk(i, a, low_rank, codes, scales)
-                if following and a == 2:
                     next_codes, next_scales = quantise_h(grouped)
             if following:
                 u_t, codes, scales = next_u_t, next_codes, next_scales

@@ -44,7 +44,7 @@ def tile_loratacmlp4_pb_kernel(tc, h, z, u, b, W_out_words, W_out_scales, b_out,
         work = ctx.enter_context(tc.tile_pool(name="work", bufs=3))
         addends = ctx.enter_context(tc.tile_pool(name="addends", bufs=2 * CHUNKS))
         results = ctx.enter_context(tc.tile_pool(name="results", bufs=12))
-        psum = ctx.enter_context(tc.psum_pool(name="psum", bufs=2))
+        psum = ctx.enter_context(tc.psum_pool(name="psum", bufs=4))
         ctx.enter_context(tc.manual_schedule())
 
         warm_in = resident.tile([P, 1], F32)
@@ -122,8 +122,8 @@ def tile_loratacmlp4_pb_kernel(tc, h, z, u, b, W_out_words, W_out_scales, b_out,
 
         def transpose_quarter(i, quarter, banks, grouped, u_t):
             if quarter % 2 == 0:
-                banks["ut"] = psum.tile([P, 2, LANES, P], BF16, name="ut")
-                banks["ht"] = psum.tile([P, 2, PAIR, P], F32, name="ht")
+                banks["ht"] = psum.tile([P, 2, PAIR, P], F32, name="ht", tag="shared")
+                banks["ut"] = psum.tile([P, 2, LANES, P], BF16, name="ut", tag="shared")
             transpose_h(i, quarter, banks["ht"])
             transpose_u(i, quarter, banks["ut"])
             if quarter % 2 == 1:
@@ -174,7 +174,7 @@ def tile_loratacmlp4_pb_kernel(tc, h, z, u, b, W_out_words, W_out_scales, b_out,
             return added
 
         def multiply_mx(i, a, added, codes, scales):
-            acc = psum.tile([P, N_CHUNK], F32)
+            acc = psum.tile([P, N_CHUNK], F32, tag="shared")
             for g in range(PASSES):
                 nc.tensor.matmul_mx(
                     out=acc[:],
@@ -193,14 +193,13 @@ def tile_loratacmlp4_pb_kernel(tc, h, z, u, b, W_out_words, W_out_scales, b_out,
 
         banks = {}
         grouped, u_t = new_stage_tiles()
-        zt = psum.tile([P, ROW_TILES, P], BF16, tag="acc")
+        zt = psum.tile([P, ROW_TILES, P], BF16, tag="shared")
+        for i in range(ROW_TILES):
+            nc.tensor.transpose(zt[:, i, :], z_sb[:, i, :], ident_bf16[:])
         z_t = resident.tile([P, ROW_TILES, P], BF16)
+        nc.scalar.copy(out=z_t[:], in_=zt[:])
         for quarter in range(CHUNKS):
             spread_bias(*divmod(2 * quarter, CHUNKS))
-            for i in (2 * quarter, 2 * quarter + 1):
-                nc.tensor.transpose(zt[:, i, :], z_sb[:, i, :], ident_bf16[:])
-            if quarter == CHUNKS - 1:
-                nc.scalar.copy(out=z_t[:], in_=zt[:])
             spread_bias(*divmod(2 * quarter + 1, CHUNKS))
             transpose_quarter(0, quarter, banks, grouped, u_t)
         codes, scales = quantise_h(grouped)

@@ -50,9 +50,10 @@ def tile_loratacmlp4_pb_kernel(tc, h, z, u, b, W_out_words, W_out_scales, b_out,
         warm_in = resident.tile([P, 1], F32)
         nc.vector.memset(warm_in[:], 0.0)
         bias_rows = resident.tile([P, BATCHES, OUT_CH], BF16)
-        nc.vector.memset(bias_rows[:].bitcast(F32), 0.0)
         ones = resident.tile([P, P], BF16)
+        nc.vector.memset(bias_rows[:, 0, :].bitcast(F32), 0.0)
         nc.vector.memset(ones[:], 1.0)
+        nc.vector.memset(bias_rows[:, 1, :].bitcast(F32), 0.0)
         w_planes = resident.tile([P, PASSES, OUT_CH], U8, align_bytes=64)
         nc.vector.memset(w_planes[:].bitcast(I32), 0)
         ident_bf16 = resident.tile([P, P], BF16)
@@ -64,9 +65,6 @@ def tile_loratacmlp4_pb_kernel(tc, h, z, u, b, W_out_words, W_out_scales, b_out,
         nc.scalar.dma_start(out=z_sb[:], in_=z.rearrange("b k f r -> f (b k) r"))
         warm_out = resident.tile([P, 1], F32)
         nc.scalar.activation(out=warm_out[:], in_=warm_in[:], func=GELU)
-        for bb in range(BATCHES):
-            nc.scalar.dma_start(out=bias_rows[0:1, bb, :], in_=b_out.unsqueeze(0))
-        nc.scalar.dma_start(out=bias_rows[1:2, :, :], in_=b.rearrange("b x y n -> (x y) b n"))
 
         h_sb = [resident.tile([P, IN_CH], BF16, name="h_sb%d" % i) for i in range(ROW_TILES)]
         u_sb = [resident.tile([P, CHUNKS, LANES, RANK], BF16, name="u_sb%d" % i) for i in range(ROW_TILES)]
@@ -74,6 +72,10 @@ def tile_loratacmlp4_pb_kernel(tc, h, z, u, b, W_out_words, W_out_scales, b_out,
             resident.tile([P, PASSES, 2 * N_CHUNK], U8, name="w_words%d" % a, align_bytes=64)
             for a in range(CHUNKS)
         ]
+
+        def load_bias_rows(bb):
+            nc.sync.dma_start(out=bias_rows[0:1, bb, :], in_=b_out.unsqueeze(0))
+            nc.sync.dma_start(out=bias_rows[1:2, bb, :], in_=b[bb].rearrange("x y n -> (x y) n"))
 
         def load_rows(i):
             nc.sync.dma_start(out=h_sb[i][:], in_=h_rows[i])
@@ -93,7 +95,9 @@ def tile_loratacmlp4_pb_kernel(tc, h, z, u, b, W_out_words, W_out_scales, b_out,
                         in_=rows[4 * quadrant + r : 16 : 8, :, :],
                     )
 
+        load_bias_rows(0)
         load_rows(0)
+        load_bias_rows(1)
         load_rows(1)
         load_weight_scales()
         for a in range(CHUNKS):
@@ -106,15 +110,18 @@ def tile_loratacmlp4_pb_kernel(tc, h, z, u, b, W_out_words, W_out_scales, b_out,
             u_t = stage.tile([P, CHUNKS, LANES, P], BF16)
             return grouped, u_t
 
+        sorted_words = {}
+
+        def sort_h(i):
+            sorted_words[i] = stage.tile([P, PASSES, PAIR, P], F32, name="sorted_words")
+            nc.scalar.copy(
+                out=sorted_words[i][:],
+                in_=h_sb[i][:].bitcast(F32).rearrange("f (g p w) -> f g w p", g=PASSES, w=PAIR),
+            )
+
         def transpose_h(i, g, ht):
-            words = h_sb[i][:].bitcast(F32)
-            per_pass = K_PASS // PAIR
             for w in range(PAIR):
-                nc.tensor.transpose(
-                    ht[:, g % 2, w, :],
-                    words[:, per_pass * g + w : per_pass * (g + 1) : PAIR],
-                    ident_f32[:],
-                )
+                nc.tensor.transpose(ht[:, g % 2, w, :], sorted_words[i][:, g, w, :], ident_f32[:])
 
         def transpose_u(i, a, ut):
             for j in range(LANES):
@@ -132,6 +139,8 @@ def tile_loratacmlp4_pb_kernel(tc, h, z, u, b, W_out_words, W_out_scales, b_out,
                     out=grouped[:].bitcast(F32)[:, quarter - 1 : quarter + 1, :, :],
                     in_=banks["ht"][:].rearrange("p g w f -> p g f w"),
                 )
+            if quarter == 1 and i + 1 < ROW_TILES:
+                sort_h(i + 1)
 
         def quantise_h(grouped):
             codes = stage.tile([P, PASSES * P], U32, align_bytes=64)
@@ -192,15 +201,17 @@ def tile_loratacmlp4_pb_kernel(tc, h, z, u, b, W_out_words, W_out_scales, b_out,
             nc.sync.dma_start(out=out_rows[i][:, a * N_CHUNK : (a + 1) * N_CHUNK], in_=result[:])
 
         banks = {}
+        sort_h(0)
         grouped, u_t = new_stage_tiles()
-        zt = psum.tile([P, ROW_TILES, P], BF16, tag="shared")
-        for i in range(ROW_TILES):
-            nc.tensor.transpose(zt[:, i, :], z_sb[:, i, :], ident_bf16[:])
         z_t = resident.tile([P, ROW_TILES, P], BF16)
-        nc.scalar.copy(out=z_t[:], in_=zt[:])
         for quarter in range(CHUNKS):
             spread_bias(*divmod(2 * quarter, CHUNKS))
             spread_bias(*divmod(2 * quarter + 1, CHUNKS))
+            if quarter == 0:
+                zt = psum.tile([P, ROW_TILES, P], BF16, tag="shared")
+                for i in range(ROW_TILES):
+                    nc.tensor.transpose(zt[:, i, :], z_sb[:, i, :], ident_bf16[:])
+                nc.scalar.copy(out=z_t[:], in_=zt[:])
             transpose_quarter(0, quarter, banks, grouped, u_t)
         codes, scales = quantise_h(grouped)
         for i in range(ROW_TILES):

@@ -43,7 +43,7 @@ def tile_loratacmlp4_pb_kernel(tc, h, z, u, b, W_out_words, W_out_scales, b_out,
         stage = ctx.enter_context(tc.tile_pool(name="stage", bufs=2))
         work = ctx.enter_context(tc.tile_pool(name="work", bufs=3))
         addends = ctx.enter_context(tc.tile_pool(name="addends", bufs=2 * CHUNKS))
-        results = ctx.enter_context(tc.tile_pool(name="results", bufs=12))
+        results = ctx.enter_context(tc.tile_pool(name="results", bufs=3 * CHUNKS))
         psum = ctx.enter_context(tc.psum_pool(name="psum", bufs=4))
         ctx.enter_context(tc.manual_schedule())
 
@@ -114,10 +114,9 @@ def tile_loratacmlp4_pb_kernel(tc, h, z, u, b, W_out_words, W_out_scales, b_out,
 
         def sort_h(i):
             sorted_words[i] = stage.tile([P, PASSES, PAIR, P], F32, name="sorted_words")
-            nc.scalar.copy(
-                out=sorted_words[i][:],
-                in_=h_sb[i][:].bitcast(F32).rearrange("f (g p w) -> f g w p", g=PASSES, w=PAIR),
-            )
+            words = h_sb[i][:].bitcast(F32).rearrange("f (g p w) -> f g w p", g=PASSES, w=PAIR)
+            for g in range(PASSES):
+                nc.gpsimd.tensor_copy(out=sorted_words[i][:, g, :, :], in_=words[:, g, :, :])
 
         def transpose_h(i, g, ht):
             for w in range(PAIR):
@@ -134,11 +133,11 @@ def tile_loratacmlp4_pb_kernel(tc, h, z, u, b, W_out_words, W_out_scales, b_out,
             transpose_h(i, quarter, banks["ht"])
             transpose_u(i, quarter, banks["ut"])
             if quarter % 2 == 1:
-                nc.scalar.copy(out=u_t[:, quarter - 1 : quarter + 1, :, :], in_=banks["ut"][:])
                 nc.scalar.copy(
                     out=grouped[:].bitcast(F32)[:, quarter - 1 : quarter + 1, :, :],
                     in_=banks["ht"][:].rearrange("p g w f -> p g f w"),
                 )
+                nc.scalar.copy(out=u_t[:, quarter - 1 : quarter + 1, :, :], in_=banks["ut"][:])
             if quarter == 1 and i + 1 < ROW_TILES:
                 sort_h(i + 1)
 
@@ -214,17 +213,18 @@ def tile_loratacmlp4_pb_kernel(tc, h, z, u, b, W_out_words, W_out_scales, b_out,
                 nc.scalar.copy(out=z_t[:], in_=zt[:])
             transpose_quarter(0, quarter, banks, grouped, u_t)
         codes, scales = quantise_h(grouped)
+
         for i in range(ROW_TILES):
             following = i + 1 < ROW_TILES
             if following:
                 grouped, next_u_t = new_stage_tiles()
-            added = []
+            added_tiles = []
             for a in range(CHUNKS):
-                added.append(multiply_low_rank(i, a, z_t, u_t))
+                added_tiles.append(multiply_low_rank(i, a, z_t, u_t))
                 if following:
                     transpose_quarter(i + 1, a, banks, grouped, next_u_t)
             for a in range(CHUNKS):
-                multiply_mx(i, a, added[a], codes, scales)
+                multiply_mx(i, a, added_tiles[a], codes, scales)
                 if following and a == 0:
                     next_codes, next_scales = quantise_h(grouped)
             if following:

@@ -32,6 +32,12 @@ PAIR = 2
 FLOPS = 2 * ROW_TILES * P * OUT_CH * (IN_CH + RANK)
 
 
+GROUP = 8
+ROW_BUFS = 4
+LR_PIECES = 1
+TAIL_PIECES = 1
+
+
 def tile_loratacmlp4_pb_kernel(tc, h, z, u, b, W_out_words, W_out_scales, b_out, out):
     nc = tc.nc
     h_rows = h.rearrange("b k f c -> (b k) f c")
@@ -40,11 +46,13 @@ def tile_loratacmlp4_pb_kernel(tc, h, z, u, b, W_out_words, W_out_scales, b_out,
 
     with ExitStack() as ctx:
         resident = ctx.enter_context(tc.tile_pool(name="resident", bufs=1))
+        rows = ctx.enter_context(tc.tile_pool(name="rows", bufs=ROW_BUFS))
         stage = ctx.enter_context(tc.tile_pool(name="stage", bufs=2))
+        kept = ctx.enter_context(tc.tile_pool(name="kept", bufs=GROUP + 1))
         work = ctx.enter_context(tc.tile_pool(name="work", bufs=3))
-        addends = ctx.enter_context(tc.tile_pool(name="addends", bufs=2 * CHUNKS))
-        results = ctx.enter_context(tc.tile_pool(name="results", bufs=3 * CHUNKS))
-        psum = ctx.enter_context(tc.psum_pool(name="psum", bufs=4))
+        addends = ctx.enter_context(tc.tile_pool(name="addends", bufs=(GROUP + 1) * CHUNKS))
+        results = ctx.enter_context(tc.tile_pool(name="results", bufs=8))
+        psum = ctx.enter_context(tc.psum_pool(name="psum", bufs=8))
         ctx.enter_context(tc.manual_schedule())
 
         warm_in = resident.tile([P, 1], F32)
@@ -66,51 +74,59 @@ def tile_loratacmlp4_pb_kernel(tc, h, z, u, b, W_out_words, W_out_scales, b_out,
         warm_out = resident.tile([P, 1], F32)
         nc.scalar.activation(out=warm_out[:], in_=warm_in[:], func=GELU)
 
-        h_sb = [resident.tile([P, IN_CH], BF16, name="h_sb%d" % i) for i in range(ROW_TILES)]
-        u_sb = [resident.tile([P, CHUNKS, LANES, RANK], BF16, name="u_sb%d" % i) for i in range(ROW_TILES)]
+        h_sb = {}
+        u_sb = {}
         w_words = [
             resident.tile([P, PASSES, 2 * N_CHUNK], U8, name="w_words%d" % a, align_bytes=64)
             for a in range(CHUNKS)
         ]
 
-        def load_bias_rows(bb):
-            nc.sync.dma_start(out=bias_rows[0:1, bb, :], in_=b_out.unsqueeze(0))
-            nc.sync.dma_start(out=bias_rows[1:2, bb, :], in_=b[bb].rearrange("x y n -> (x y) n"))
-
         def load_rows(i):
+            if i < BATCHES:
+                nc.sync.dma_start(out=bias_rows[0:1, i, :], in_=b_out.unsqueeze(0))
+                nc.sync.dma_start(out=bias_rows[1:2, i, :], in_=b[i].rearrange("x y n -> (x y) n"))
+            h_sb[i] = rows.tile([P, IN_CH], BF16, name="h_sb")
+            u_sb[i] = rows.tile([P, CHUNKS, LANES, RANK], BF16, name="u_sb")
             nc.sync.dma_start(out=h_sb[i][:], in_=h_rows[i])
             nc.sync.dma_start(out=u_sb[i][:], in_=u_rows[i])
 
-        def load_weight_chunk(a):
-            words = W_out_words.bitcast(I32).rearrange("g p n -> p g n")
-            width = 2 * N_CHUNK // 4
-            nc.sync.dma_start(out=w_words[a][:].bitcast(I32), in_=words[:, :, a * width : (a + 1) * width])
-
-        def load_weight_scales():
-            rows = W_out_scales.bitcast(I32).rearrange("g q n -> q g n")
+        def load_weight():
+            rows_q = W_out_scales.bitcast(I32).rearrange("g q n -> q g n")
             for quadrant in range(2):
                 for r in range(4):
                     nc.sync.dma_start(
                         out=w_planes[32 * quadrant + r : P : 64, :, :].bitcast(I32),
-                        in_=rows[4 * quadrant + r : 16 : 8, :, :],
+                        in_=rows_q[4 * quadrant + r : 16 : 8, :, :],
                     )
+            words = W_out_words.bitcast(I32).rearrange("g p n -> p g n")
+            width = 2 * N_CHUNK // 4
+            for a in range(CHUNKS):
+                nc.sync.dma_start(out=w_words[a][:].bitcast(I32), in_=words[:, :, a * width : (a + 1) * width])
 
-        load_bias_rows(0)
-        load_rows(0)
-        load_bias_rows(1)
-        load_rows(1)
-        load_weight_scales()
-        for a in range(CHUNKS):
-            load_weight_chunk(a)
-        for i in range(2, ROW_TILES):
-            load_rows(i)
+        WEIGHT = -1
+        last_before_weight = min(GROUP, ROW_TILES - 1)
+        plan = list(range(last_before_weight + 1)) + [WEIGHT] + list(range(last_before_weight + 1, ROW_TILES))
+        issued = {"n": 0}
 
-        def new_stage_tiles():
-            grouped = stage.tile([P, PASSES, P, PACK], BF16, align_bytes=64)
-            u_t = stage.tile([P, CHUNKS, LANES, P], BF16)
-            return grouped, u_t
+        def issue_loads(limit):
+            while issued["n"] < len(plan) and plan[issued["n"]] <= limit:
+                item = plan[issued["n"]]
+                issued["n"] = issued["n"] + 1
+                if item == WEIGHT:
+                    load_weight()
+                else:
+                    load_rows(item)
 
+        issue_loads(ROW_BUFS - 1)
+
+        grouped = {}
+        u_t = {}
         sorted_words = {}
+        banks = {}
+        bias = {}
+        added = {}
+        codes = {}
+        scales = {}
 
         def sort_h(i):
             sorted_words[i] = stage.tile([P, PASSES, PAIR, P], F32, name="sorted_words")
@@ -118,114 +134,134 @@ def tile_loratacmlp4_pb_kernel(tc, h, z, u, b, W_out_words, W_out_scales, b_out,
             for g in range(PASSES):
                 nc.gpsimd.tensor_copy(out=sorted_words[i][:, g, :, :], in_=words[:, g, :, :])
 
-        def transpose_h(i, g, ht):
-            for w in range(PAIR):
-                nc.tensor.transpose(ht[:, g % 2, w, :], sorted_words[i][:, g, w, :], ident_f32[:])
+        def transposes_of(i):
+            ops = []
+            for quarter in range(CHUNKS):
+                for w in range(PAIR):
+                    ops.append(("h", quarter, w))
+                for j in range(LANES):
+                    ops.append(("u", quarter, j))
+            return ops
 
-        def transpose_u(i, a, ut):
-            for j in range(LANES):
-                nc.tensor.transpose(ut[:, a % 2, j, :], u_sb[i][:, a, j, :], ident_bf16[:])
+        def transpose_one(i, kind, quarter, index):
+            if kind == "h" and index == 0 and quarter == 0:
+                grouped[i] = kept.tile([P, PASSES, P, PACK], BF16, name="grouped", align_bytes=64)
+                u_t[i] = stage.tile([P, CHUNKS, LANES, P], BF16, name="u_t")
+            if kind == "h":
+                if index == 0 and quarter % 2 == 0:
+                    banks["ht"] = psum.tile([P, 2, PAIR, P], F32, name="ht", tag="bank")
+                nc.tensor.transpose(banks["ht"][:, quarter % 2, index, :], sorted_words[i][:, quarter, index, :], ident_f32[:])
+            else:
+                if index == 0 and quarter % 2 == 0:
+                    banks["ut"] = psum.tile([P, 2, LANES, P], BF16, name="ut", tag="bank")
+                nc.tensor.transpose(banks["ut"][:, quarter % 2, index, :], u_sb[i][:, quarter, index, :], ident_bf16[:])
+                if index == LANES - 1 and quarter % 2 == 1:
+                    nc.scalar.copy(
+                        out=grouped[i][:].bitcast(F32)[:, quarter - 1 : quarter + 1, :, :],
+                        in_=banks["ht"][:].rearrange("p g w f -> p g f w"),
+                    )
+                    nc.scalar.copy(out=u_t[i][:, quarter - 1 : quarter + 1, :, :], in_=banks["ut"][:])
+                if index == LANES - 1 and quarter == 1 and i + 1 < ROW_TILES:
+                    sort_h(i + 1)
+                if index == LANES - 1 and quarter == CHUNKS - 1:
+                    issue_loads(i + ROW_BUFS)
 
-        def transpose_quarter(i, quarter, banks, grouped, u_t):
-            if quarter % 2 == 0:
-                banks["ht"] = psum.tile([P, 2, PAIR, P], F32, name="ht", tag="shared")
-                banks["ut"] = psum.tile([P, 2, LANES, P], BF16, name="ut", tag="shared")
-            transpose_h(i, quarter, banks["ht"])
-            transpose_u(i, quarter, banks["ut"])
-            if quarter % 2 == 1:
-                nc.scalar.copy(
-                    out=grouped[:].bitcast(F32)[:, quarter - 1 : quarter + 1, :, :],
-                    in_=banks["ht"][:].rearrange("p g w f -> p g f w"),
-                )
-                nc.scalar.copy(out=u_t[:, quarter - 1 : quarter + 1, :, :], in_=banks["ut"][:])
-            if quarter == 1 and i + 1 < ROW_TILES:
-                sort_h(i + 1)
-
-        def quantise_h(grouped):
-            codes = stage.tile([P, PASSES * P], U32, align_bytes=64)
-            scales = stage.tile([P, PASSES * P], U8, align_bytes=64)
+        def quantise_h(i):
+            codes[i] = stage.tile([P, PASSES * P], U32, name="codes", align_bytes=64)
+            scales[i] = stage.tile([P, PASSES * P], U8, name="scales", align_bytes=64)
             nc.vector.quantize_mx(
-                out=codes[:].bitcast(FP8X4),
-                scales=scales[:],
-                in_=grouped[:].rearrange("p g f t -> p (g f t)"),
+                out=codes[i][:].bitcast(FP8X4),
+                scales=scales[i][:],
+                in_=grouped[i][:].rearrange("p g f t -> p (g f t)"),
             )
-            return codes, scales
-
-        bias = {}
 
         def spread_bias(bb, a):
-            spread = psum.tile([P, N_CHUNK], F32, tag="low_rank")
+            spread = psum.tile([P, N_CHUNK], F32, name="spread", tag="bank")
             nc.tensor.matmul(
                 spread[:], lhsT=ones[:], rhs=bias_rows[:, bb, a * N_CHUNK : (a + 1) * N_CHUNK], start=True, stop=True
             )
             bias[bb, a] = resident.tile([P, N_CHUNK], F32, name="bias%d_%d" % (bb, a))
             nc.vector.tensor_copy(out=bias[bb, a][:], in_=spread[:])
 
-        def multiply_low_rank(i, a, z_t, u_t):
-            low_rank = psum.tile([P, N_CHUNK], F32)
+        def low_rank_piece(i, a, s):
+            if s == 0:
+                banks["lr"] = psum.tile([P, N_CHUNK], F32, name="low_rank", tag="bank")
+            width = N_CHUNK // LR_PIECES
             nc.tensor.matmul(
-                low_rank[:],
+                banks["lr"][:, s * width : (s + 1) * width],
                 lhsT=z_t[:, i, :],
-                rhs=u_t[:, a, :, :].rearrange("r j p -> r (j p)"),
+                rhs=u_t[i][:, a, :, :].rearrange("r j p -> r (j p)")[:, s * width : (s + 1) * width],
                 start=True,
                 stop=True,
             )
-            added = addends.tile([P, N_CHUNK], F32)
-            nc.vector.scalar_tensor_tensor(
-                out=added[:].rearrange("f (p j) -> f p j", j=LANES),
-                in0=low_rank[:].rearrange("f (j p) -> f p j", j=LANES),
-                scalar=1.0 / RANK,
-                in1=bias[i // MEMBERS, a][:].rearrange("f (p j) -> f p j", j=LANES),
-                op0=MULT,
-                op1=ADD,
-            )
-            return added
-
-        def multiply_mx(i, a, added, codes, scales):
-            acc = psum.tile([P, N_CHUNK], F32, tag="shared")
-            for g in range(PASSES):
-                nc.tensor.matmul_mx(
-                    out=acc[:],
-                    lhsT=codes[:, g * P : (g + 1) * P].bitcast(FP8X4),
-                    lhsT_scale=scales[:, g * P : (g + 1) * P],
-                    rhs=w_words[a][:, g, :].bitcast(FP4X4),
-                    rhs_scale=w_planes[:, g, a * N_CHUNK : (a + 1) * N_CHUNK],
-                    start=(g == 0),
-                    stop=(g == PASSES - 1),
+            if s == LR_PIECES - 1:
+                added[i, a] = addends.tile([P, N_CHUNK], F32, name="added")
+                nc.vector.scalar_tensor_tensor(
+                    out=added[i, a][:].rearrange("f (p j) -> f p j", j=LANES),
+                    in0=banks["lr"][:].rearrange("f (j p) -> f p j", j=LANES),
+                    scalar=1.0 / RANK,
+                    in1=bias[i // MEMBERS, a][:].rearrange("f (p j) -> f p j", j=LANES),
+                    op0=MULT,
+                    op1=ADD,
                 )
-            total = work.tile([P, N_CHUNK], F32)
-            nc.vector.tensor_tensor(out=total[:], in0=acc[:], in1=added[:], op=ADD)
-            result = results.tile([P, N_CHUNK], F32)
-            nc.scalar.activation(out=result[:], in_=total[:], func=GELU)
-            nc.sync.dma_start(out=out_rows[i][:, a * N_CHUNK : (a + 1) * N_CHUNK], in_=result[:])
 
-        banks = {}
+        def multiply_mx(i, a, pieces):
+            width = N_CHUNK // pieces
+            for s in range(pieces):
+                lo = s * width
+                acc = psum.tile([P, width], F32, name="acc", tag="bank")
+                for g in range(PASSES):
+                    nc.tensor.matmul_mx(
+                        out=acc[:],
+                        lhsT=codes[i][:, g * P : (g + 1) * P].bitcast(FP8X4),
+                        lhsT_scale=scales[i][:, g * P : (g + 1) * P],
+                        rhs=w_words[a][:, g, 2 * lo : 2 * (lo + width)].bitcast(FP4X4),
+                        rhs_scale=w_planes[:, g, a * N_CHUNK + lo : a * N_CHUNK + lo + width],
+                        start=(g == 0),
+                        stop=(g == PASSES - 1),
+                    )
+                total = work.tile([P, width], F32, name="total")
+                nc.vector.tensor_tensor(out=total[:], in0=acc[:], in1=added[i, a][:, lo : lo + width], op=ADD)
+                result = results.tile([P, width], F32, name="result")
+                nc.scalar.activation(out=result[:], in_=total[:], func=GELU)
+                nc.sync.dma_start(out=out_rows[i][:, a * N_CHUNK + lo : a * N_CHUNK + lo + width], in_=result[:])
+
+        def plain_step(i):
+            pieces = [(a, s) for a in range(CHUNKS) for s in range(LR_PIECES)]
+            turns = transposes_of(i + 1) if i + 1 < ROW_TILES else []
+            share = len(turns) // len(pieces)
+            extra = len(turns) - share * len(pieces)
+            at = 0
+            for n, (a, s) in enumerate(pieces):
+                low_rank_piece(i, a, s)
+                count = share + (1 if n % 2 == 1 and n // 2 < extra else 0)
+                for kind, quarter, index in turns[at : at + count]:
+                    transpose_one(i + 1, kind, quarter, index)
+                at = at + count
+            assert at == len(turns)
+
         sort_h(0)
-        grouped, u_t = new_stage_tiles()
         z_t = resident.tile([P, ROW_TILES, P], BF16)
+        first = transposes_of(0)
+        per_quarter = len(first) // CHUNKS
         for quarter in range(CHUNKS):
             spread_bias(*divmod(2 * quarter, CHUNKS))
             spread_bias(*divmod(2 * quarter + 1, CHUNKS))
             if quarter == 0:
-                zt = psum.tile([P, ROW_TILES, P], BF16, tag="shared")
+                zt = psum.tile([P, ROW_TILES, P], BF16, name="zt", tag="bank")
                 for i in range(ROW_TILES):
                     nc.tensor.transpose(zt[:, i, :], z_sb[:, i, :], ident_bf16[:])
                 nc.scalar.copy(out=z_t[:], in_=zt[:])
-            transpose_quarter(0, quarter, banks, grouped, u_t)
-        codes, scales = quantise_h(grouped)
+            for kind, q, index in first[quarter * per_quarter : (quarter + 1) * per_quarter]:
+                transpose_one(0, kind, q, index)
+        quantise_h(0)
 
-        for i in range(ROW_TILES):
-            following = i + 1 < ROW_TILES
-            if following:
-                grouped, next_u_t = new_stage_tiles()
-            added_tiles = []
-            for a in range(CHUNKS):
-                added_tiles.append(multiply_low_rank(i, a, z_t, u_t))
-                if following:
-                    transpose_quarter(i + 1, a, banks, grouped, next_u_t)
-            for a in range(CHUNKS):
-                multiply_mx(i, a, added_tiles[a], codes, scales)
-                if following and a == 0:
-                    next_codes, next_scales = quantise_h(grouped)
-            if following:
-                u_t, codes, scales = next_u_t, next_codes, next_scales
+        for start in range(0, ROW_TILES, GROUP):
+            for i in range(start, start + GROUP):
+                plain_step(i)
+            for i in range(start, start + GROUP):
+                for a in range(CHUNKS):
+                    last = i == ROW_TILES - 1 and a == CHUNKS - 1
+                    multiply_mx(i, a, TAIL_PIECES if last else 1)
+                    if a == 0 and i + 1 < ROW_TILES:
+                        quantise_h(i + 1)

@@ -35,7 +35,8 @@ FLOPS = 2 * ROW_TILES * P * OUT_CH * (IN_CH + RANK)
 GROUP = 8
 ROW_BUFS = 4
 LR_PIECES = 1
-TAIL_PIECES = 1
+TAIL_PIECES = 4
+WARM = 6
 
 
 def tile_loratacmlp4_pb_kernel(tc, h, z, u, b, W_out_words, W_out_scales, b_out, out):
@@ -59,8 +60,10 @@ def tile_loratacmlp4_pb_kernel(tc, h, z, u, b, W_out_words, W_out_scales, b_out,
         nc.vector.memset(warm_in[:], 0.0)
         bias_rows = resident.tile([P, BATCHES, OUT_CH], BF16)
         ones = resident.tile([P, P], BF16)
+        warm_rhs = resident.tile([P, N_CHUNK], BF16)
+        nc.gpsimd.memset(ones[:], 1.0)
+        nc.gpsimd.memset(warm_rhs[:].bitcast(F32), 0.0)
         nc.vector.memset(bias_rows[:, 0, :].bitcast(F32), 0.0)
-        nc.vector.memset(ones[:], 1.0)
         nc.vector.memset(bias_rows[:, 1, :].bitcast(F32), 0.0)
         w_planes = resident.tile([P, PASSES, OUT_CH], U8, align_bytes=64)
         nc.vector.memset(w_planes[:].bitcast(I32), 0)
@@ -160,7 +163,10 @@ def tile_loratacmlp4_pb_kernel(tc, h, z, u, b, W_out_words, W_out_scales, b_out,
                         out=grouped[i][:].bitcast(F32)[:, quarter - 1 : quarter + 1, :, :],
                         in_=banks["ht"][:].rearrange("p g w f -> p g f w"),
                     )
-                    nc.scalar.copy(out=u_t[i][:, quarter - 1 : quarter + 1, :, :], in_=banks["ut"][:])
+                    nc.scalar.copy(
+                        out=u_t[i][:, quarter - 1 : quarter + 1, :, :].rearrange("r a j p -> r (a j p)").bitcast(F32),
+                        in_=banks["ut"][:].rearrange("r a j p -> r (a j p)").bitcast(F32),
+                    )
                 if index == LANES - 1 and quarter == 1 and i + 1 < ROW_TILES:
                     sort_h(i + 1)
                 if index == LANES - 1 and quarter == CHUNKS - 1:
@@ -242,18 +248,21 @@ def tile_loratacmlp4_pb_kernel(tc, h, z, u, b, W_out_words, W_out_scales, b_out,
 
         sort_h(0)
         z_t = resident.tile([P, ROW_TILES, P], BF16)
+        warm_bank = psum.tile([P, N_CHUNK], F32, name="warm_bank", tag="bank")
+        for n in range(WARM):
+            nc.tensor.matmul(warm_bank[:], lhsT=ones[:], rhs=warm_rhs[:], start=True, stop=True)
+        for a in range(CHUNKS):
+            spread_bias(0, a)
+        zt = psum.tile([P, ROW_TILES, P], BF16, name="zt", tag="bank")
+        for i in range(ROW_TILES):
+            nc.tensor.transpose(zt[:, i, :], z_sb[:, i, :], ident_bf16[:])
+        nc.scalar.copy(out=z_t[:], in_=zt[:])
         first = transposes_of(0)
         per_quarter = len(first) // CHUNKS
         for quarter in range(CHUNKS):
-            spread_bias(*divmod(2 * quarter, CHUNKS))
-            spread_bias(*divmod(2 * quarter + 1, CHUNKS))
-            if quarter == 0:
-                zt = psum.tile([P, ROW_TILES, P], BF16, name="zt", tag="bank")
-                for i in range(ROW_TILES):
-                    nc.tensor.transpose(zt[:, i, :], z_sb[:, i, :], ident_bf16[:])
-                nc.scalar.copy(out=z_t[:], in_=zt[:])
             for kind, q, index in first[quarter * per_quarter : (quarter + 1) * per_quarter]:
                 transpose_one(0, kind, q, index)
+            spread_bias(1, quarter)
         quantise_h(0)
 
         for start in range(0, ROW_TILES, GROUP):

@@ -37,21 +37,22 @@ ROW_BUFS = 4
 LR_PIECES = 1
 TAIL_PIECES = 4
 WARM = 6
+ORDER = "quarters"
 
 
 def tile_loratacmlp4_pb_kernel(tc, h, z, u, b, W_out_words, W_out_scales, b_out, out):
     nc = tc.nc
     h_rows = h.rearrange("b k f c -> (b k) f c")
     out_rows = out.rearrange("b k f n -> (b k) f n")
-    u_rows = u.rearrange("b k (a p j) r -> (b k) p a j r", a=CHUNKS, p=P)
+    u_rows = u.rearrange("b k (p a j) r -> (b k) p a j r", a=CHUNKS, p=P)
 
     with ExitStack() as ctx:
         resident = ctx.enter_context(tc.tile_pool(name="resident", bufs=1))
         rows = ctx.enter_context(tc.tile_pool(name="rows", bufs=ROW_BUFS))
         stage = ctx.enter_context(tc.tile_pool(name="stage", bufs=2))
-        kept = ctx.enter_context(tc.tile_pool(name="kept", bufs=GROUP + 1))
+        kept = ctx.enter_context(tc.tile_pool(name="kept", bufs=min(GROUP + 1, ROW_TILES)))
         work = ctx.enter_context(tc.tile_pool(name="work", bufs=3))
-        addends = ctx.enter_context(tc.tile_pool(name="addends", bufs=(GROUP + 1) * CHUNKS))
+        addends = ctx.enter_context(tc.tile_pool(name="addends", bufs=min(GROUP + 1, ROW_TILES)))
         results = ctx.enter_context(tc.tile_pool(name="results", bufs=8))
         psum = ctx.enter_context(tc.psum_pool(name="psum", bufs=8))
         ctx.enter_context(tc.manual_schedule())
@@ -139,11 +140,19 @@ def tile_loratacmlp4_pb_kernel(tc, h, z, u, b, W_out_words, W_out_scales, b_out,
 
         def transposes_of(i):
             ops = []
-            for quarter in range(CHUNKS):
-                for w in range(PAIR):
-                    ops.append(("h", quarter, w))
-                for j in range(LANES):
-                    ops.append(("u", quarter, j))
+            if ORDER == "quarters":
+                for quarter in range(CHUNKS):
+                    for w in range(PAIR):
+                        ops.append(("h", quarter, w))
+                    for j in range(LANES):
+                        ops.append(("u", quarter, j))
+            else:
+                for quarter in range(CHUNKS):
+                    for w in range(PAIR):
+                        ops.append(("h", quarter, w))
+                for quarter in range(CHUNKS):
+                    for j in range(LANES):
+                        ops.append(("u", quarter, j))
             return ops
 
         def transpose_one(i, kind, quarter, index):
@@ -154,15 +163,16 @@ def tile_loratacmlp4_pb_kernel(tc, h, z, u, b, W_out_words, W_out_scales, b_out,
                 if index == 0 and quarter % 2 == 0:
                     banks["ht"] = psum.tile([P, 2, PAIR, P], F32, name="ht", tag="bank")
                 nc.tensor.transpose(banks["ht"][:, quarter % 2, index, :], sorted_words[i][:, quarter, index, :], ident_f32[:])
+                if index == PAIR - 1 and quarter % 2 == 1:
+                    nc.scalar.copy(
+                        out=grouped[i][:].bitcast(F32)[:, quarter - 1 : quarter + 1, :, :],
+                        in_=banks["ht"][:].rearrange("p g w f -> p g f w"),
+                    )
             else:
                 if index == 0 and quarter % 2 == 0:
                     banks["ut"] = psum.tile([P, 2, LANES, P], BF16, name="ut", tag="bank")
                 nc.tensor.transpose(banks["ut"][:, quarter % 2, index, :], u_sb[i][:, quarter, index, :], ident_bf16[:])
                 if index == LANES - 1 and quarter % 2 == 1:
-                    nc.scalar.copy(
-                        out=grouped[i][:].bitcast(F32)[:, quarter - 1 : quarter + 1, :, :],
-                        in_=banks["ht"][:].rearrange("p g w f -> p g f w"),
-                    )
                     nc.scalar.copy(
                         out=u_t[i][:, quarter - 1 : quarter + 1, :, :].rearrange("r a j p -> r (a j p)").bitcast(F32),
                         in_=banks["ut"][:].rearrange("r a j p -> r (a j p)").bitcast(F32),
@@ -186,8 +196,9 @@ def tile_loratacmlp4_pb_kernel(tc, h, z, u, b, W_out_words, W_out_scales, b_out,
             nc.tensor.matmul(
                 spread[:], lhsT=ones[:], rhs=bias_rows[:, bb, a * N_CHUNK : (a + 1) * N_CHUNK], start=True, stop=True
             )
-            bias[bb, a] = resident.tile([P, N_CHUNK], F32, name="bias%d_%d" % (bb, a))
-            nc.vector.tensor_copy(out=bias[bb, a][:], in_=spread[:])
+            if a == 0:
+                bias[bb] = resident.tile([P, OUT_CH], F32, name="bias%d" % bb)
+            nc.vector.tensor_copy(out=bias[bb][:, a * N_CHUNK : (a + 1) * N_CHUNK], in_=spread[:])
 
         def low_rank_piece(i, a, s):
             if s == 0:
@@ -201,12 +212,13 @@ def tile_loratacmlp4_pb_kernel(tc, h, z, u, b, W_out_words, W_out_scales, b_out,
                 stop=True,
             )
             if s == LR_PIECES - 1:
-                added[i, a] = addends.tile([P, N_CHUNK], F32, name="added")
+                if a == 0:
+                    added[i] = addends.tile([P, OUT_CH], F32, name="added")
                 nc.vector.scalar_tensor_tensor(
-                    out=added[i, a][:].rearrange("f (p j) -> f p j", j=LANES),
+                    out=added[i][:].rearrange("f (p a j) -> f a p j", a=CHUNKS, j=LANES)[:, a, :, :],
                     in0=banks["lr"][:].rearrange("f (j p) -> f p j", j=LANES),
                     scalar=1.0 / RANK,
-                    in1=bias[i // MEMBERS, a][:].rearrange("f (p j) -> f p j", j=LANES),
+                    in1=bias[i // MEMBERS][:].rearrange("f (p a j) -> f a p j", a=CHUNKS, j=LANES)[:, a, :, :],
                     op0=MULT,
                     op1=ADD,
                 )
@@ -227,7 +239,7 @@ def tile_loratacmlp4_pb_kernel(tc, h, z, u, b, W_out_words, W_out_scales, b_out,
                         stop=(g == PASSES - 1),
                     )
                 total = work.tile([P, width], F32, name="total")
-                nc.vector.tensor_tensor(out=total[:], in0=acc[:], in1=added[i, a][:, lo : lo + width], op=ADD)
+                nc.vector.tensor_tensor(out=total[:], in0=acc[:], in1=added[i][:, a * N_CHUNK + lo : a * N_CHUNK + lo + width], op=ADD)
                 result = results.tile([P, width], F32, name="result")
                 nc.scalar.activation(out=result[:], in_=total[:], func=GELU)
                 nc.sync.dma_start(out=out_rows[i][:, a * N_CHUNK + lo : a * N_CHUNK + lo + width], in_=result[:])
@@ -238,13 +250,19 @@ def tile_loratacmlp4_pb_kernel(tc, h, z, u, b, W_out_words, W_out_scales, b_out,
             share = len(turns) // len(pieces)
             extra = len(turns) - share * len(pieces)
             at = 0
+            if ORDER == "runs":
+                for kind, quarter, index in turns:
+                    transpose_one(i + 1, kind, quarter, index)
+                at = len(turns)
+                turns = []
             for n, (a, s) in enumerate(pieces):
                 low_rank_piece(i, a, s)
                 count = share + (1 if n % 2 == 1 and n // 2 < extra else 0)
+                if ORDER == "runs":
+                    count = 0
                 for kind, quarter, index in turns[at : at + count]:
                     transpose_one(i + 1, kind, quarter, index)
                 at = at + count
-            assert at == len(turns)
 
         sort_h(0)
         z_t = resident.tile([P, ROW_TILES, P], BF16)

@@ -244,6 +244,27 @@ def tile_loratacmlp4_pb_kernel(tc, h, z, u, b, W_out_words, W_out_scales, b_out,
                 nc.scalar.activation(out=result[:], in_=total[:], func=GELU)
                 nc.sync.dma_start(out=out_rows[i][:, a * N_CHUNK + lo : a * N_CHUNK + lo + width], in_=result[:])
 
+        def multiply_mx_by_pass(i):
+            accs = [psum.tile([P, N_CHUNK], F32, name="acc", tag="bank") for a in range(CHUNKS)]
+            for g in range(PASSES):
+                for a in range(CHUNKS):
+                    nc.tensor.matmul_mx(
+                        out=accs[a][:],
+                        lhsT=codes[i][:, g * P : (g + 1) * P].bitcast(FP8X4),
+                        lhsT_scale=scales[i][:, g * P : (g + 1) * P],
+                        rhs=w_words[a][:, g, :].bitcast(FP4X4),
+                        rhs_scale=w_planes[:, g, a * N_CHUNK : (a + 1) * N_CHUNK],
+                        start=(g == 0),
+                        stop=(g == PASSES - 1),
+                    )
+            quantise_h(i + 1)
+            for a in range(CHUNKS):
+                total = work.tile([P, N_CHUNK], F32, name="total")
+                nc.vector.tensor_tensor(out=total[:], in0=accs[a][:], in1=added[i][:, a * N_CHUNK : (a + 1) * N_CHUNK], op=ADD)
+                result = results.tile([P, N_CHUNK], F32, name="result")
+                nc.scalar.activation(out=result[:], in_=total[:], func=GELU)
+                nc.sync.dma_start(out=out_rows[i][:, a * N_CHUNK : (a + 1) * N_CHUNK], in_=result[:])
+
         def plain_step(i):
             pieces = [(a, s) for a in range(CHUNKS) for s in range(LR_PIECES)]
             turns = transposes_of(i + 1) if i + 1 < ROW_TILES else []
@@ -287,8 +308,9 @@ def tile_loratacmlp4_pb_kernel(tc, h, z, u, b, W_out_words, W_out_scales, b_out,
             for i in range(start, start + GROUP):
                 plain_step(i)
             for i in range(start, start + GROUP):
+                if i + 1 < ROW_TILES:
+                    multiply_mx_by_pass(i)
+                    continue
                 for a in range(CHUNKS):
                     last = i == ROW_TILES - 1 and a == CHUNKS - 1
                     multiply_mx(i, a, TAIL_PIECES if last else 1)
-                    if a == 0 and i + 1 < ROW_TILES:
-                        quantise_h(i + 1)

@@ -308,9 +308,11 @@ def tile_loratacmlp4_pb_kernel(tc, h, z, u, b, W_out_words, W_out_scales, b_out,
             for i in range(start, start + GROUP):
                 plain_step(i)
             for i in range(start, start + GROUP):
-                if i + 1 < ROW_TILES:
+                if 0 < i < ROW_TILES - 1:
                     multiply_mx_by_pass(i)
                     continue
                 for a in range(CHUNKS):
                     last = i == ROW_TILES - 1 and a == CHUNKS - 1
                     multiply_mx(i, a, TAIL_PIECES if last else 1)
+                    if a == 0 and i + 1 < ROW_TILES:
+                        quantise_h(i + 1)

from contextlib import ExitStack

import concourse.mybir as mybir
from concourse.masks import make_identity

BF16 = mybir.dt.bfloat16
F32 = mybir.dt.float32
I32 = mybir.dt.int32
U8 = mybir.dt.uint8
U32 = mybir.dt.uint32
FP8X4 = mybir.dt.float8_e4m3fn_x4
FP4X4 = mybir.dt.float4_e2m1fn_x4
ADD = mybir.AluOpType.add
MULT = mybir.AluOpType.mult
GELU = mybir.ActivationFunctionType.Gelu

P = 128
BATCHES = 2
MEMBERS = 4
ROW_TILES = BATCHES * MEMBERS
IN_CH = 2048
OUT_CH = 2048
RANK = 128
PACK = 4
K_PASS = P * PACK
PASSES = IN_CH // K_PASS
N_CHUNK = 512
CHUNKS = OUT_CH // N_CHUNK
LANES = N_CHUNK // P
PAIR = 2

FLOPS = 2 * ROW_TILES * P * OUT_CH * (IN_CH + RANK)


GROUP = 8
ROW_BUFS = 4
LR_PIECES = 1
TAIL_PIECES = 4
WARM = 6
ORDER = "quarters"


def tile_loratacmlp4_pb_kernel(tc, h, z, u, b, W_out_words, W_out_scales, b_out, out):
    nc = tc.nc
    h_rows = h.rearrange("b k f c -> (b k) f c")
    out_rows = out.rearrange("b k f n -> (b k) f n")
    u_rows = u.rearrange("b k (p a j) r -> (b k) p a j r", a=CHUNKS, p=P)

    with ExitStack() as ctx:
        resident = ctx.enter_context(tc.tile_pool(name="resident", bufs=1))
        rows = ctx.enter_context(tc.tile_pool(name="rows", bufs=ROW_BUFS))
        stage = ctx.enter_context(tc.tile_pool(name="stage", bufs=2))
        kept = ctx.enter_context(tc.tile_pool(name="kept", bufs=min(GROUP + 1, ROW_TILES)))
        work = ctx.enter_context(tc.tile_pool(name="work", bufs=3))
        addends = ctx.enter_context(tc.tile_pool(name="addends", bufs=min(GROUP + 1, ROW_TILES)))
        results = ctx.enter_context(tc.tile_pool(name="results", bufs=8))
        psum = ctx.enter_context(tc.psum_pool(name="psum", bufs=8))
        ctx.enter_context(tc.manual_schedule())

        warm_in = resident.tile([P, 1], F32)
        nc.vector.memset(warm_in[:], 0.0)
        bias_rows = resident.tile([P, BATCHES, OUT_CH], BF16)
        ones = resident.tile([P, P], BF16)
        warm_rhs = resident.tile([P, N_CHUNK], BF16)
        nc.gpsimd.memset(ones[:], 1.0)
        nc.gpsimd.memset(warm_rhs[:].bitcast(F32), 0.0)
        nc.vector.memset(bias_rows[:, 0, :].bitcast(F32), 0.0)
        nc.vector.memset(bias_rows[:, 1, :].bitcast(F32), 0.0)
        w_planes = resident.tile([P, PASSES, OUT_CH], U8, align_bytes=64)
        nc.vector.memset(w_planes[:].bitcast(I32), 0)
        ident_bf16 = resident.tile([P, P], BF16)
        make_identity(nc, ident_bf16[:])
        ident_f32 = resident.tile([P, P], F32)
        make_identity(nc, ident_f32[:])

        z_sb = resident.tile([P, ROW_TILES, RANK], BF16)
        nc.scalar.dma_start(out=z_sb[:], in_=z.rearrange("b k f r -> f (b k) r"))
        warm_out = resident.tile([P, 1], F32)
        nc.scalar.activation(out=warm_out[:], in_=warm_in[:], func=GELU)

        h_sb = {}
        u_sb = {}
        w_words = [
            resident.tile([P, PASSES, 2 * N_CHUNK], U8, name="w_words%d" % a, align_bytes=64)
            for a in range(CHUNKS)
        ]

        def load_rows(i):
            if i < BATCHES:
                nc.sync.dma_start(out=bias_rows[0:1, i, :], in_=b_out.unsqueeze(0))
                nc.sync.dma_start(out=bias_rows[1:2, i, :], in_=b[i].rearrange("x y n -> (x y) n"))
            h_sb[i] = rows.tile([P, IN_CH], BF16, name="h_sb")
            u_sb[i] = rows.tile([P, CHUNKS, LANES, RANK], BF16, name="u_sb")
            nc.sync.dma_start(out=h_sb[i][:], in_=h_rows[i])
            nc.sync.dma_start(out=u_sb[i][:], in_=u_rows[i])

        def load_weight():
            rows_q = W_out_scales.bitcast(I32).rearrange("g q n -> q g n")
            for quadrant in range(2):
                for r in range(4):
                    nc.sync.dma_start(
                        out=w_planes[32 * quadrant + r : P : 64, :, :].bitcast(I32),
                        in_=rows_q[4 * quadrant + r : 16 : 8, :, :],
                    )
            words = W_out_words.bitcast(I32).rearrange("g p n -> p g n")
            width = 2 * N_CHUNK // 4
            for a in range(CHUNKS):
                nc.sync.dma_start(out=w_words[a][:].bitcast(I32), in_=words[:, :, a * width : (a + 1) * width])

        WEIGHT = -1
        last_before_weight = min(GROUP, ROW_TILES - 1)
        plan = list(range(last_before_weight + 1)) + [WEIGHT] + list(range(last_before_weight + 1, ROW_TILES))
        issued = {"n": 0}

        def issue_loads(limit):
            while issued["n"] < len(plan) and plan[issued["n"]] <= limit:
                item = plan[issued["n"]]
                issued["n"] = issued["n"] + 1
                if item == WEIGHT:
                    load_weight()
                else:
                    load_rows(item)

        issue_loads(ROW_BUFS - 1)

        grouped = {}
        u_t = {}
        sorted_words = {}
        banks = {}
        bias = {}
        added = {}
        codes = {}
        scales = {}

        def sort_h(i):
            sorted_words[i] = stage.tile([P, PASSES, PAIR, P], F32, name="sorted_words")
            words = h_sb[i][:].bitcast(F32).rearrange("f (g p w) -> f g w p", g=PASSES, w=PAIR)
            for g in range(PASSES):
                nc.gpsimd.tensor_copy(out=sorted_words[i][:, g, :, :], in_=words[:, g, :, :])

        def transposes_of(i):
            ops = []
            if ORDER == "quarters":
                for quarter in range(CHUNKS):
                    for w in range(PAIR):
                        ops.append(("h", quarter, w))
                    for j in range(LANES):
                        ops.append(("u", quarter, j))
            else:
                for quarter in range(CHUNKS):
                    for w in range(PAIR):
                        ops.append(("h", quarter, w))
                for quarter in range(CHUNKS):
                    for j in range(LANES):
                        ops.append(("u", quarter, j))
            return ops

        def transpose_one(i, kind, quarter, index):
            if kind == "h" and index == 0 and quarter == 0:
                grouped[i] = kept.tile([P, PASSES, P, PACK], BF16, name="grouped", align_bytes=64)
                u_t[i] = stage.tile([P, CHUNKS, LANES, P], BF16, name="u_t")
            if kind == "h":
                if index == 0 and quarter % 2 == 0:
                    banks["ht"] = psum.tile([P, 2, PAIR, P], F32, name="ht", tag="bank")
                nc.tensor.transpose(banks["ht"][:, quarter % 2, index, :], sorted_words[i][:, quarter, index, :], ident_f32[:])
                if index == PAIR - 1 and quarter % 2 == 1:
                    nc.scalar.copy(
                        out=grouped[i][:].bitcast(F32)[:, quarter - 1 : quarter + 1, :, :],
                        in_=banks["ht"][:].rearrange("p g w f -> p g f w"),
                    )
            else:
                if index == 0 and quarter % 2 == 0:
                    banks["ut"] = psum.tile([P, 2, LANES, P], BF16, name="ut", tag="bank")
                nc.tensor.transpose(banks["ut"][:, quarter % 2, index, :], u_sb[i][:, quarter, index, :], ident_bf16[:])
                if index == LANES - 1 and quarter % 2 == 1:
                    nc.scalar.copy(
                        out=u_t[i][:, quarter - 1 : quarter + 1, :, :].rearrange("r a j p -> r (a j p)").bitcast(F32),
                        in_=banks["ut"][:].rearrange("r a j p -> r (a j p)").bitcast(F32),
                    )
                if index == LANES - 1 and quarter == 1 and i + 1 < ROW_TILES:
                    sort_h(i + 1)
                if index == LANES - 1 and quarter == CHUNKS - 1:
                    issue_loads(i + ROW_BUFS)

        def quantise_h(i):
            codes[i] = stage.tile([P, PASSES * P], U32, name="codes", align_bytes=64)
            scales[i] = stage.tile([P, PASSES * P], U8, name="scales", align_bytes=64)
            nc.vector.quantize_mx(
                out=codes[i][:].bitcast(FP8X4),
                scales=scales[i][:],
                in_=grouped[i][:].rearrange("p g f t -> p (g f t)"),
            )

        def spread_bias(bb, a):
            spread = psum.tile([P, N_CHUNK], F32, name="spread", tag="bank")
            nc.tensor.matmul(
                spread[:], lhsT=ones[:], rhs=bias_rows[:, bb, a * N_CHUNK : (a + 1) * N_CHUNK], start=True, stop=True
            )
            if a == 0:
                bias[bb] = resident.tile([P, OUT_CH], F32, name="bias%d" % bb)
            nc.vector.tensor_copy(out=bias[bb][:, a * N_CHUNK : (a + 1) * N_CHUNK], in_=spread[:])

        def low_rank_piece(i, a, s):
            if s == 0:
                banks["lr"] = psum.tile([P, N_CHUNK], F32, name="low_rank", tag="bank")
            width = N_CHUNK // LR_PIECES
            nc.tensor.matmul(
                banks["lr"][:, s * width : (s + 1) * width],
                lhsT=z_t[:, i, :],
                rhs=u_t[i][:, a, :, :].rearrange("r j p -> r (j p)")[:, s * width : (s + 1) * width],
                start=True,
                stop=True,
            )
            if s == LR_PIECES - 1:
                if a == 0:
                    added[i] = addends.tile([P, OUT_CH], F32, name="added")
                nc.vector.scalar_tensor_tensor(
                    out=added[i][:].rearrange("f (p a j) -> f a p j", a=CHUNKS, j=LANES)[:, a, :, :],
                    in0=banks["lr"][:].rearrange("f (j p) -> f p j", j=LANES),
                    scalar=1.0 / RANK,
                    in1=bias[i // MEMBERS][:].rearrange("f (p a j) -> f a p j", a=CHUNKS, j=LANES)[:, a, :, :],
                    op0=MULT,
                    op1=ADD,
                )

        def multiply_mx(i, a, pieces):
            width = N_CHUNK // pieces
            for s in range(pieces):
                lo = s * width
                acc = psum.tile([P, width], F32, name="acc", tag="bank")
                for g in range(PASSES):
                    nc.tensor.matmul_mx(
                        out=acc[:],
                        lhsT=codes[i][:, g * P : (g + 1) * P].bitcast(FP8X4),
                        lhsT_scale=scales[i][:, g * P : (g + 1) * P],
                        rhs=w_words[a][:, g, 2 * lo : 2 * (lo + width)].bitcast(FP4X4),
                        rhs_scale=w_planes[:, g, a * N_CHUNK + lo : a * N_CHUNK + lo + width],
                        start=(g == 0),
                        stop=(g == PASSES - 1),
                    )
                total = work.tile([P, width], F32, name="total")
                nc.vector.tensor_tensor(out=total[:], in0=acc[:], in1=added[i][:, a * N_CHUNK + lo : a * N_CHUNK + lo + width], op=ADD)
                result = results.tile([P, width], F32, name="result")
                nc.scalar.activation(out=result[:], in_=total[:], func=GELU)
                nc.sync.dma_start(out=out_rows[i][:, a * N_CHUNK + lo : a * N_CHUNK + lo + width], in_=result[:])

        def multiply_mx_by_pass(i):
            accs = [psum.tile([P, N_CHUNK], F32, name="acc", tag="bank") for a in range(CHUNKS)]
            for g in range(PASSES):
                for a in range(CHUNKS):
                    nc.tensor.matmul_mx(
                        out=accs[a][:],
                        lhsT=codes[i][:, g * P : (g + 1) * P].bitcast(FP8X4),
                        lhsT_scale=scales[i][:, g * P : (g + 1) * P],
                        rhs=w_words[a][:, g, :].bitcast(FP4X4),
                        rhs_scale=w_planes[:, g, a * N_CHUNK : (a + 1) * N_CHUNK],
                        start=(g == 0),
                        stop=(g == PASSES - 1),
                    )
            quantise_h(i + 1)
            for a in range(CHUNKS):
                total = work.tile([P, N_CHUNK], F32, name="total")
                nc.vector.tensor_tensor(out=total[:], in0=accs[a][:], in1=added[i][:, a * N_CHUNK : (a + 1) * N_CHUNK], op=ADD)
                result = results.tile([P, N_CHUNK], F32, name="result")
                nc.scalar.activation(out=result[:], in_=total[:], func=GELU)
                nc.sync.dma_start(out=out_rows[i][:, a * N_CHUNK : (a + 1) * N_CHUNK], in_=result[:])

        def plain_step(i):
            pieces = [(a, s) for a in range(CHUNKS) for s in range(LR_PIECES)]
            turns = transposes_of(i + 1) if i + 1 < ROW_TILES else []
            share = len(turns) // len(pieces)
            extra = len(turns) - share * len(pieces)
            at = 0
            if ORDER == "runs":
                for kind, quarter, index in turns:
                    transpose_one(i + 1, kind, quarter, index)
                at = len(turns)
                turns = []
            for n, (a, s) in enumerate(pieces):
                low_rank_piece(i, a, s)
                count = share + (1 if n % 2 == 1 and n // 2 < extra else 0)
                if ORDER == "runs":
                    count = 0
                for kind, quarter, index in turns[at : at + count]:
                    transpose_one(i + 1, kind, quarter, index)
                at = at + count

        sort_h(0)
        z_t = resident.tile([P, ROW_TILES, P], BF16)
        warm_bank = psum.tile([P, N_CHUNK], F32, name="warm_bank", tag="bank")
        for n in range(WARM):
            nc.tensor.matmul(warm_bank[:], lhsT=ones[:], rhs=warm_rhs[:], start=True, stop=True)
        for a in range(CHUNKS):
            spread_bias(0, a)
        zt = psum.tile([P, ROW_TILES, P], BF16, name="zt", tag="bank")
        for i in range(ROW_TILES):
            nc.tensor.transpose(zt[:, i, :], z_sb[:, i, :], ident_bf16[:])
        nc.scalar.copy(out=z_t[:], in_=zt[:])
        first = transposes_of(0)
        per_quarter = len(first) // CHUNKS
        for quarter in range(CHUNKS):
            for kind, q, index in first[quarter * per_quarter : (quarter + 1) * per_quarter]:
                transpose_one(0, kind, q, index)
            spread_bias(1, quarter)
        quantise_h(0)

        for start in range(0, ROW_TILES, GROUP):
            for i in range(start, start + GROUP):
                plain_step(i)
            for i in range(start, start + GROUP):
                if 0 < i < ROW_TILES - 1:
                    multiply_mx_by_pass(i)
                    continue
                for a in range(CHUNKS):
                    last = i == ROW_TILES - 1 and a == CHUNKS - 1
                    multiply_mx(i, a, TAIL_PIECES if last else 1)
                    if a == 0 and i + 1 < ROW_TILES:
                        quantise_h(i + 1)
